import numpy as np
import ml_dtypes


def mxq(x, axis, fmt="e4m3"):
    dtype, down = {"e4m3": (ml_dtypes.float8_e4m3fn, 7), "e5m2": (ml_dtypes.float8_e5m2, 14)}[fmt]
    v = np.moveaxis(np.asarray(x, np.float32).astype(ml_dtypes.bfloat16).astype(np.float64), axis, -1)
    blocks = v.reshape(v.shape[:-1] + (-1, 32))
    amax = np.abs(blocks).max(-1, keepdims=True)
    byte = np.maximum(np.where(amax > 0, np.frexp(amax)[1] - 1 + 127, 0) - down, 1)
    scale = np.exp2(byte - 127.0)
    codes = (blocks / scale).astype(np.float32).astype(dtype).astype(np.float64)
    return np.moveaxis((codes * scale).reshape(v.shape), -1, axis)


WIDE = False


def mx_kscale(k):
    if not WIDE:
        return np.ones(k)
    levels = np.array([10, -10, 5, -5, 0])
    a = np.random.permutation(np.resize(levels, k // 512 * 4)).reshape(k // 512, 4)
    idx = np.arange(k)
    return np.exp2(a[idx // 512, idx % 128 // 32])


BF16 = ml_dtypes.bfloat16


def bf(x):
    return np.asarray(x, np.float32).astype(BF16)


def f64(x):
    return np.asarray(x).astype(np.float64)


B, N, F, L, R = 128, 1024, 1024, 128, 16
SIGMA_DEC = 1.0


def rbf_gram(a, b, sigma):
    sq = (np.sum(a * a, axis=-1)[:, None]
          + np.sum(b * b, axis=-1)[None, :]
          - 2.0 * (a @ b.T))
    sq = np.maximum(sq, 0.0)
    return np.exp(-sq / (2.0 * sigma * sigma))


def setup_inputs():
    t = mx_kscale(N)
    t = t / t.max()
    c = np.random.standard_normal((N, L)) * 1.4 / np.sqrt(L)
    n2 = np.sum(c * c, axis=1)
    c = c * np.sqrt((n2 + 2.0 * np.log(1.0 / t)) / n2)[:, None]
    return {"z": bf(np.random.standard_normal((B, L)) * 1.4 / np.sqrt(L)), "centers_decoder": bf(c),
            "alpha_decoder": bf(np.random.standard_normal((N, F)) * 7.0 / np.sqrt(N) / t[:, None])}


def reference(z, centers_decoder, alpha_decoder):
    k_dec = rbf_gram(f64(z), f64(centers_decoder), SIGMA_DEC)
    return mxq(k_dec, 1, "e4m3") @ mxq(f64(alpha_decoder), 0, "e4m3")

@@ -1,0 +1,188 @@
+from contextlib import ExitStack
+
+import concourse.mybir as mybir
+from concourse.masks import make_identity
+
+BF16 = mybir.dt.bfloat16
+F32 = mybir.dt.float32
+U32 = mybir.dt.uint32
+U8 = mybir.dt.uint8
+FP8X4 = mybir.dt.float8_e4m3fn_x4
+ALU = mybir.AluOpType
+ACT = mybir.ActivationFunctionType
+
+P = 128
+PACK = 4
+K_PASS = P * PACK
+SAMPLES = 128
+LATENT = 128
+CENTRES = 1024
+FEATURES = 1024
+PASSES = CENTRES // K_PASS
+F_TILE = 512
+F_TILES = FEATURES // F_TILE
+RUN = 4
+SCALAR_COLS = 192
+
+FLOPS = 2 * SAMPLES * LATENT * CENTRES + 2 * SAMPLES * CENTRES * FEATURES
+
+
+def side_by_side(rows, grouped):
+    return (
+        rows.rearrange("p t (w i) -> p w t i", i=RUN),
+        grouped.rearrange("p (w i) t -> p w t i", i=RUN),
+    )
+
+
+def tile_autoencoder_pb_s_kernel(tc, z, centers_decoder, alpha_decoder, out):
+    nc = tc.nc
+    blocks = PASSES * PACK
+    vector_cols = slice(0, F_TILE - SCALAR_COLS)
+    scalar_cols = slice(F_TILE - SCALAR_COLS, F_TILE)
+    with ExitStack() as ctx:
+        keep = ctx.enter_context(tc.tile_pool(name="keep", bufs=1))
+        psum = ctx.enter_context(tc.psum_pool(name="psum", bufs=1))
+        ctx.enter_context(tc.manual_schedule())
+
+        z_sb = keep.tile([P, LATENT], BF16)
+        c_sb = keep.tile([P, blocks, LATENT], BF16)
+        a_rows = keep.tile([P, F_TILES, PASSES, PACK, F_TILE], BF16)
+        a_grouped = keep.tile([P, F_TILES, PASSES, F_TILE, PACK], BF16, align_bytes=64)
+        a_codes = keep.tile([P, F_TILES, PASSES, F_TILE], U32, align_bytes=64)
+        a_scales = keep.tile([P, F_TILES, PASSES, F_TILE], U8, align_bytes=64)
+        k_rows = keep.tile([P, PASSES, PACK, SAMPLES], BF16)
+        k_grouped = keep.tile([P, PASSES, SAMPLES, PACK], BF16, align_bytes=64)
+        k_codes = keep.tile([P, PASSES, SAMPLES], U32, align_bytes=64)
+        k_scales = keep.tile([P, PASSES, SAMPLES], U8, align_bytes=64)
+        sq = keep.tile([P, PASSES, PACK, SAMPLES], F32)
+        result = keep.tile([P, F_TILES, F_TILE], F32)
+
+        nc.sync.dma_start(out=z_sb[:], in_=z)
+        nc.sync.dma_start(
+            out=c_sb[:].rearrange("p (c t) l -> p c (t l)", c=PASSES),
+            in_=centers_decoder.rearrange("(c p t) l -> p c (t l)", c=PASSES, t=PACK),
+        )
+        for f in range(F_TILES):
+            for c in range(PASSES):
+                nc.sync.dma_start(
+                    out=a_rows[:, f, c, :, :],
+                    in_=alpha_decoder[
+                        c * K_PASS : (c + 1) * K_PASS, f * F_TILE : (f + 1) * F_TILE
+                    ].rearrange("(p t) w -> p t w", t=PACK),
+                )
+
+        def regroup_alpha(f, c):
+            src, dst = side_by_side(
+                a_rows[:, f, c, :, vector_cols], a_grouped[:, f, c, vector_cols, :]
+            )
+            nc.vector.tensor_copy(out=dst, in_=src)
+            src, dst = side_by_side(
+                a_rows[:, f, c, :, scalar_cols], a_grouped[:, f, c, scalar_cols, :]
+            )
+            nc.scalar.copy(out=dst, in_=src)
+
+        def quantise_alpha(f, c):
+            nc.vector.quantize_mx(
+                out=a_codes[:, f, c, :].bitcast(FP8X4),
+                scales=a_scales[:, f, c, :],
+                in_=a_grouped[:, f, c, :, :].rearrange("p w t -> p (w t)"),
+            )
+
+        def multiply(acc, f, c):
+            nc.tensor.matmul_mx(
+                out=acc,
+                lhsT=k_codes[:, c, :].bitcast(FP8X4),
+                lhsT_scale=k_scales[:, c, :],
+                rhs=a_codes[:, f, c, :].bitcast(FP8X4),
+                rhs_scale=a_scales[:, f, c, :],
+                start=(c == 0),
+                stop=(c == PASSES - 1),
+            )
+
+        ident_bf = keep.tile([P, P], BF16)
+        make_identity(nc, ident_bf[:])
+        ident_f32 = keep.tile([P, P], F32)
+        make_identity(nc, ident_f32[:])
+        zero_col = keep.tile([P, 1], F32)
+        nc.vector.memset(zero_col[:], 0.0)
+        one_col = keep.tile([P, 1], F32)
+        nc.scalar.activation(out=one_col[:], in_=zero_col[:], func=ACT.Exp)
+
+        zz = keep.tile([P, 1], F32)
+        z_sq = keep.tile([P, LATENT], F32)
+        nc.scalar.activation(out=z_sq[:], in_=z_sb[:], func=ACT.Square, accum_out=zz[:])
+        zT_ps = psum.tile([P, SAMPLES], BF16)
+        nc.tensor.transpose(zT_ps[:], z_sb[:], ident_bf[:])
+        zT_m2 = keep.tile([P, SAMPLES], BF16)
+        nc.scalar.mul(out=zT_m2[:], in_=zT_ps[:], mul=-2.0)
+
+        cT = keep.tile([P, blocks, P], BF16)
+        for c in range(PASSES):
+            cT_ps = psum.tile([P, PACK, P], BF16, name="cT_ps_%d" % c)
+            for t in range(PACK):
+                nc.tensor.transpose(cT_ps[:, t, :], c_sb[:, c * PACK + t, :], ident_bf[:])
+            nc.vector.tensor_copy(out=cT[:, c * PACK : (c + 1) * PACK, :], in_=cT_ps[:])
+        cc = keep.tile([P, blocks], F32)
+        c_sq = keep.tile([P, blocks, LATENT], F32)
+        for b in range(blocks):
+            nc.scalar.activation(
+                out=c_sq[:, b, :], in_=c_sb[:, b, :], func=ACT.Square, accum_out=cc[:, b : b + 1]
+            )
+
+        zz_ps = psum.tile([P, SAMPLES], F32)
+        nc.tensor.matmul(
+            zz_ps[:], lhsT=zz[:, 0:1].to_broadcast([P, P]), rhs=ident_f32[:], start=True, stop=True
+        )
+        zz_row = keep.tile([P, SAMPLES], F32)
+        nc.vector.tensor_copy(out=zz_row[:], in_=zz_ps[:])
+
+        regroup_alpha(0, 0)
+
+        for c in range(PASSES):
+            g_ps = psum.tile([P, PACK, SAMPLES], F32, name="g_ps_%d" % c)
+            for t in range(PACK):
+                nc.tensor.matmul(
+                    g_ps[:, t, :], lhsT=cT[:, c * PACK + t, :], rhs=zT_m2[:], start=True, stop=True
+                )
+            for t in range(PACK):
+                b = c * PACK + t
+                nc.vector.scalar_tensor_tensor(
+                    out=sq[:, c, t, :],
+                    in0=g_ps[:, t, :],
+                    scalar=cc[:, b : b + 1],
+                    in1=zz_row[:],
+                    op0=ALU.add,
+                    op1=ALU.add,
+                )
+            nc.scalar.activation(out=k_rows[:, c, :, :], in_=sq[:, c, :, :], func=ACT.Exp, scale=-0.5)
+
+        def clamp_and_regroup_k(c):
+            src, dst = side_by_side(k_rows[:, c, :, :], k_grouped[:, c, :, :])
+            nc.vector.tensor_scalar_min(out=dst, in0=src, scalar1=1.0)
+
+        quantise_alpha(0, 0)
+        clamp_and_regroup_k(0)
+        regroup_alpha(0, 1)
+        clamp_and_regroup_k(1)
+        nc.vector.quantize_mx(
+            out=k_codes[:].rearrange("p c i -> p (c i)").bitcast(FP8X4),
+            scales=k_scales[:].rearrange("p c i -> p (c i)"),
+            in_=k_grouped[:].rearrange("p c i t -> p (c i t)"),
+        )
+        quantise_alpha(0, 1)
+
+        acc_0 = psum.tile([P, F_TILE], F32)
+        multiply(acc_0[:], 0, 0)
+        multiply(acc_0[:], 0, 1)
+        regroup_alpha(1, 0)
+        regroup_alpha(1, 1)
+        nc.scalar.copy(out=result[:, 0, :], in_=acc_0[:])
+        nc.sync.dma_start(out=out[:, 0:F_TILE], in_=result[:, 0, :])
+
+        acc_1 = psum.tile([P, F_TILE], F32)
+        quantise_alpha(1, 0)
+        multiply(acc_1[:], 1, 0)
+        quantise_alpha(1, 1)
+        multiply(acc_1[:], 1, 1)
+        nc.vector.tensor_copy(out=result[:, 1, :], in_=acc_1[:])
+        nc.sync.dma_start(out=out[:, F_TILE : 2 * F_TILE], in_=result[:, 1, :])

@@ -54,7 +54,6 @@ def tile_autoencoder_pb_s_kernel(tc, z, centers_decoder, alpha_decoder, out):
         k_grouped = keep.tile([P, PASSES, SAMPLES, PACK], BF16, align_bytes=64)
         k_codes = keep.tile([P, PASSES, SAMPLES], U32, align_bytes=64)
         k_scales = keep.tile([P, PASSES, SAMPLES], U8, align_bytes=64)
-        sq = keep.tile([P, PASSES, PACK, SAMPLES], F32)
         result = keep.tile([P, F_TILES, F_TILE], F32)
 
         nc.sync.dma_start(out=z_sb[:], in_=z)
@@ -129,12 +128,8 @@ def tile_autoencoder_pb_s_kernel(tc, z, centers_decoder, alpha_decoder, out):
                 out=c_sq[:, b, :], in_=c_sb[:, b, :], func=ACT.Square, accum_out=cc[:, b : b + 1]
             )
 
-        zz_ps = psum.tile([P, SAMPLES], F32)
-        nc.tensor.matmul(
-            zz_ps[:], lhsT=zz[:, 0:1].to_broadcast([P, P]), rhs=ident_f32[:], start=True, stop=True
-        )
-        zz_row = keep.tile([P, SAMPLES], F32)
-        nc.vector.tensor_copy(out=zz_row[:], in_=zz_ps[:])
+        ncc = keep.tile([P, blocks], F32)
+        nc.scalar.mul(out=ncc[:], in_=cc[:], mul=-0.5)
 
         regroup_alpha(0, 0)
 
@@ -142,19 +137,25 @@ def tile_autoencoder_pb_s_kernel(tc, z, centers_decoder, alpha_decoder, out):
             g_ps = psum.tile([P, PACK, SAMPLES], F32, name="g_ps_%d" % c)
             for t in range(PACK):
                 nc.tensor.matmul(
-                    g_ps[:, t, :], lhsT=cT[:, c * PACK + t, :], rhs=zT_m2[:], start=True, stop=True
+                    g_ps[:, t, :], lhsT=cT[:, c * PACK + t, :], rhs=zT_m2[:], start=True, stop=False
+                )
+                nc.tensor.matmul(
+                    g_ps[:, t, :],
+                    lhsT=zz[:, 0:1].to_broadcast([P, P]),
+                    rhs=ident_f32[:],
+                    start=False,
+                    stop=True,
+                    is_transpose=True,
                 )
             for t in range(PACK):
                 b = c * PACK + t
-                nc.vector.scalar_tensor_tensor(
-                    out=sq[:, c, t, :],
-                    in0=g_ps[:, t, :],
-                    scalar=cc[:, b : b + 1],
-                    in1=zz_row[:],
-                    op0=ALU.add,
-                    op1=ALU.add,
+                nc.scalar.activation(
+                    out=k_rows[:, c, t, :],
+                    in_=g_ps[:, t, :],
+                    func=ACT.Exp,
+                    scale=-0.5,
+                    bias=ncc[:, b : b + 1],
                 )
-            nc.scalar.activation(out=k_rows[:, c, :, :], in_=sq[:, c, :, :], func=ACT.Exp, scale=-0.5)
 
         def clamp_and_regroup_k(c):
             src, dst = side_by_side(k_rows[:, c, :, :], k_grouped[:, c, :, :])

@@ -19,10 +19,19 @@ LATENT = 128
 CENTRES = 1024
 FEATURES = 1024
 PASSES = CENTRES // K_PASS
+BLOCKS = PASSES * PACK
 F_TILE = 512
 F_TILES = FEATURES // F_TILE
 RUN = 4
-SCALAR_COLS = 192
+VECTOR_NORMS = 3
+
+UNITS = (
+    (0, 0, 0, 512, 288),
+    (0, 1, 0, 512, 288),
+    (1, 0, 0, 512, 288),
+    (1, 1, 0, 256, 96),
+    (1, 1, 256, 512, 256),
+)
 
 FLOPS = 2 * SAMPLES * LATENT * CENTRES + 2 * SAMPLES * CENTRES * FEATURES
 
@@ -36,16 +45,13 @@ def side_by_side(rows, grouped):
 
 def tile_autoencoder_pb_s_kernel(tc, z, centers_decoder, alpha_decoder, out):
     nc = tc.nc
-    blocks = PASSES * PACK
-    vector_cols = slice(0, F_TILE - SCALAR_COLS)
-    scalar_cols = slice(F_TILE - SCALAR_COLS, F_TILE)
     with ExitStack() as ctx:
         keep = ctx.enter_context(tc.tile_pool(name="keep", bufs=1))
         psum = ctx.enter_context(tc.psum_pool(name="psum", bufs=1))
         ctx.enter_context(tc.manual_schedule())
 
         z_sb = keep.tile([P, LATENT], BF16)
-        c_sb = keep.tile([P, blocks, LATENT], BF16)
+        c_sb = keep.tile([P, BLOCKS, LATENT], BF16)
         a_rows = keep.tile([P, F_TILES, PASSES, PACK, F_TILE], BF16)
         a_grouped = keep.tile([P, F_TILES, PASSES, F_TILE, PACK], BF16, align_bytes=64)
         a_codes = keep.tile([P, F_TILES, PASSES, F_TILE], U32, align_bytes=64)
@@ -54,13 +60,16 @@ def tile_autoencoder_pb_s_kernel(tc, z, centers_decoder, alpha_decoder, out):
         k_grouped = keep.tile([P, PASSES, SAMPLES, PACK], BF16, align_bytes=64)
         k_codes = keep.tile([P, PASSES, SAMPLES], U32, align_bytes=64)
         k_scales = keep.tile([P, PASSES, SAMPLES], U8, align_bytes=64)
-        result = keep.tile([P, F_TILES, F_TILE], F32)
+        result = keep.tile([P, FEATURES], F32)
 
         nc.sync.dma_start(out=z_sb[:], in_=z)
-        nc.sync.dma_start(
-            out=c_sb[:].rearrange("p (c t) l -> p c (t l)", c=PASSES),
-            in_=centers_decoder.rearrange("(c p t) l -> p c (t l)", c=PASSES, t=PACK),
-        )
+        for c in range(PASSES):
+            nc.sync.dma_start(
+                out=c_sb[:, c * PACK : (c + 1) * PACK, :].rearrange("p t l -> p (t l)"),
+                in_=centers_decoder[c * K_PASS : (c + 1) * K_PASS, :].rearrange(
+                    "(p t) l -> p (t l)", t=PACK
+                ),
+            )
         for f in range(F_TILES):
             for c in range(PASSES):
                 nc.sync.dma_start(
@@ -70,30 +79,31 @@ def tile_autoencoder_pb_s_kernel(tc, z, centers_decoder, alpha_decoder, out):
                     ].rearrange("(p t) w -> p t w", t=PACK),
                 )
 
-        def regroup_alpha(f, c):
-            src, dst = side_by_side(
-                a_rows[:, f, c, :, vector_cols], a_grouped[:, f, c, vector_cols, :]
-            )
+        def regroup_vector(u):
+            f, c, lo, hi, v = UNITS[u]
+            src, dst = side_by_side(a_rows[:, f, c, :, lo : lo + v], a_grouped[:, f, c, lo : lo + v, :])
             nc.vector.tensor_copy(out=dst, in_=src)
-            src, dst = side_by_side(
-                a_rows[:, f, c, :, scalar_cols], a_grouped[:, f, c, scalar_cols, :]
-            )
+
+        def regroup_scalar(u):
+            f, c, lo, hi, v = UNITS[u]
+            src, dst = side_by_side(a_rows[:, f, c, :, lo + v : hi], a_grouped[:, f, c, lo + v : hi, :])
             nc.scalar.copy(out=dst, in_=src)
 
-        def quantise_alpha(f, c):
+        def quantise_alpha(u):
+            f, c, lo, hi, v = UNITS[u]
             nc.vector.quantize_mx(
-                out=a_codes[:, f, c, :].bitcast(FP8X4),
-                scales=a_scales[:, f, c, :],
-                in_=a_grouped[:, f, c, :, :].rearrange("p w t -> p (w t)"),
+                out=a_codes[:, f, c, lo:hi].bitcast(FP8X4),
+                scales=a_scales[:, f, c, lo:hi],
+                in_=a_grouped[:, f, c, lo:hi, :].rearrange("p w t -> p (w t)"),
             )
 
-        def multiply(acc, f, c):
+        def multiply(acc, f, c, lo, hi):
             nc.tensor.matmul_mx(
                 out=acc,
                 lhsT=k_codes[:, c, :].bitcast(FP8X4),
                 lhsT_scale=k_scales[:, c, :],
-                rhs=a_codes[:, f, c, :].bitcast(FP8X4),
-                rhs_scale=a_scales[:, f, c, :],
+                rhs=a_codes[:, f, c, lo:hi].bitcast(FP8X4),
+                rhs_scale=a_scales[:, f, c, lo:hi],
                 start=(c == 0),
                 stop=(c == PASSES - 1),
             )
@@ -110,80 +120,122 @@ def tile_autoencoder_pb_s_kernel(tc, z, centers_decoder, alpha_decoder, out):
         zz = keep.tile([P, 1], F32)
         z_sq = keep.tile([P, LATENT], F32)
         nc.scalar.activation(out=z_sq[:], in_=z_sb[:], func=ACT.Square, accum_out=zz[:])
-        zT_ps = psum.tile([P, SAMPLES], BF16)
+        zT_ps = psum.tile([P, SAMPLES], BF16, tag="bank_z")
         nc.tensor.transpose(zT_ps[:], z_sb[:], ident_bf[:])
         zT_m2 = keep.tile([P, SAMPLES], BF16)
         nc.scalar.mul(out=zT_m2[:], in_=zT_ps[:], mul=-2.0)
 
-        cT = keep.tile([P, blocks, P], BF16)
+        cT = keep.tile([P, BLOCKS, P], BF16)
+        cT_ps = []
         for c in range(PASSES):
-            cT_ps = psum.tile([P, PACK, P], BF16, name="cT_ps_%d" % c)
+            cT_ps.append(psum.tile([P, PACK, P], BF16, name="cT_ps_%d" % c))
             for t in range(PACK):
-                nc.tensor.transpose(cT_ps[:, t, :], c_sb[:, c * PACK + t, :], ident_bf[:])
-            nc.vector.tensor_copy(out=cT[:, c * PACK : (c + 1) * PACK, :], in_=cT_ps[:])
-        cc = keep.tile([P, blocks], F32)
-        c_sq = keep.tile([P, blocks, LATENT], F32)
-        for b in range(blocks):
+                nc.tensor.transpose(cT_ps[c][:, t, :], c_sb[:, c * PACK + t, :], ident_bf[:])
+
+        g_ps = []
+        for c in range(PASSES):
+            g_ps.append(psum.tile([P, PACK, SAMPLES], F32, name="g_ps_%d" % c))
+            for t in range(PACK):
+                nc.tensor.matmul(
+                    g_ps[c][:, t, :],
+                    lhsT=zz[:, 0:1].to_broadcast([P, P]),
+                    rhs=ident_f32[:],
+                    start=(t == 0),
+                    stop=False,
+                    is_transpose=True,
+                )
+
+        scalar_norms = BLOCKS - VECTOR_NORMS
+        cc = keep.tile([P, scalar_norms], F32)
+        ncc_s = keep.tile([P, scalar_norms], F32)
+        ncc_v = keep.tile([P, VECTOR_NORMS], F32)
+        c_sq = keep.tile([P, BLOCKS, LATENT], F32)
+        for b in range(scalar_norms):
             nc.scalar.activation(
                 out=c_sq[:, b, :], in_=c_sb[:, b, :], func=ACT.Square, accum_out=cc[:, b : b + 1]
             )
-
-        ncc = keep.tile([P, blocks], F32)
-        nc.scalar.mul(out=ncc[:], in_=cc[:], mul=-0.5)
-
-        regroup_alpha(0, 0)
+        nc.scalar.mul(out=ncc_s[:], in_=cc[:], mul=-0.5)
+        for b in range(scalar_norms, BLOCKS):
+            nc.vector.scalar_tensor_tensor(
+                out=c_sq[:, b, :],
+                in0=c_sb[:, b, :],
+                scalar=-0.5,
+                in1=c_sb[:, b, :],
+                op0=ALU.mult,
+                op1=ALU.mult,
+                accum_out=ncc_v[:, b - scalar_norms : b - scalar_norms + 1],
+            )
+        for c in range(PASSES):
+            nc.vector.tensor_copy(out=cT[:, c * PACK : (c + 1) * PACK, :], in_=cT_ps[c][:])
 
         for c in range(PASSES):
-            g_ps = psum.tile([P, PACK, SAMPLES], F32, name="g_ps_%d" % c)
             for t in range(PACK):
                 nc.tensor.matmul(
-                    g_ps[:, t, :], lhsT=cT[:, c * PACK + t, :], rhs=zT_m2[:], start=True, stop=False
-                )
-                nc.tensor.matmul(
-                    g_ps[:, t, :],
-                    lhsT=zz[:, 0:1].to_broadcast([P, P]),
-                    rhs=ident_f32[:],
+                    g_ps[c][:, t, :],
+                    lhsT=cT[:, c * PACK + t, :],
+                    rhs=zT_m2[:],
                     start=False,
-                    stop=True,
-                    is_transpose=True,
+                    stop=(t == PACK - 1),
                 )
+
+        def exp_k(c):
             for t in range(PACK):
                 b = c * PACK + t
+                bias = ncc_s[:, b : b + 1] if b < scalar_norms else ncc_v[:, b - scalar_norms : b - scalar_norms + 1]
                 nc.scalar.activation(
-                    out=k_rows[:, c, t, :],
-                    in_=g_ps[:, t, :],
-                    func=ACT.Exp,
-                    scale=-0.5,
-                    bias=ncc[:, b : b + 1],
+                    out=k_rows[:, c, t, :], in_=g_ps[c][:, t, :], func=ACT.Exp, scale=-0.5, bias=bias
                 )
 
         def clamp_and_regroup_k(c):
             src, dst = side_by_side(k_rows[:, c, :, :], k_grouped[:, c, :, :])
             nc.vector.tensor_scalar_min(out=dst, in0=src, scalar1=1.0)
 
-        quantise_alpha(0, 0)
+        def store(lo, hi):
+            nc.sync.dma_start(out=out[:, lo:hi], in_=result[:, lo:hi])
+
+        regroup_scalar(0)
+        regroup_vector(0)
+        exp_k(0)
+        regroup_vector(1)
+        regroup_scalar(1)
+        quantise_alpha(0)
+        exp_k(1)
+        regroup_vector(2)
+        regroup_scalar(2)
+        quantise_alpha(1)
         clamp_and_regroup_k(0)
-        regroup_alpha(0, 1)
         clamp_and_regroup_k(1)
+        regroup_vector(3)
+        regroup_scalar(3)
         nc.vector.quantize_mx(
             out=k_codes[:].rearrange("p c i -> p (c i)").bitcast(FP8X4),
             scales=k_scales[:].rearrange("p c i -> p (c i)"),
             in_=k_grouped[:].rearrange("p c i t -> p (c i t)"),
         )
-        quantise_alpha(0, 1)
+        quantise_alpha(2)
 
-        acc_0 = psum.tile([P, F_TILE], F32)
-        multiply(acc_0[:], 0, 0)
-        multiply(acc_0[:], 0, 1)
-        regroup_alpha(1, 0)
-        regroup_alpha(1, 1)
-        nc.scalar.copy(out=result[:, 0, :], in_=acc_0[:])
-        nc.sync.dma_start(out=out[:, 0:F_TILE], in_=result[:, 0, :])
+        acc_0 = psum.tile([P, 512], F32)
+        multiply(acc_0[:], 0, 0, 0, 512)
+        multiply(acc_0[:], 0, 1, 0, 512)
+        nc.scalar.copy(out=result[:, 0:512], in_=acc_0[:])
+        store(0, 512)
 
-        acc_1 = psum.tile([P, F_TILE], F32)
-        quantise_alpha(1, 0)
-        multiply(acc_1[:], 1, 0)
-        quantise_alpha(1, 1)
-        multiply(acc_1[:], 1, 1)
-        nc.vector.tensor_copy(out=result[:, 1, :], in_=acc_1[:])
-        nc.sync.dma_start(out=out[:, F_TILE : 2 * F_TILE], in_=result[:, 1, :])
+        regroup_vector(4)
+        quantise_alpha(3)
+        acc_1 = psum.tile([P, 256], F32)
+        acc_2 = psum.tile([P, 128], F32)
+        acc_3 = psum.tile([P, 128], F32, tag="bank_z")
+        multiply(acc_1[:], 1, 0, 0, 256)
+        multiply(acc_2[:], 1, 0, 256, 384)
+        multiply(acc_3[:], 1, 0, 384, 512)
+        multiply(acc_1[:], 1, 1, 0, 256)
+        nc.scalar.copy(out=result[:, 512:768], in_=acc_1[:])
+        store(512, 768)
+
+        quantise_alpha(4)
+        multiply(acc_2[:], 1, 1, 256, 384)
+        multiply(acc_3[:], 1, 1, 384, 512)
+        nc.vector.tensor_copy(out=result[:, 768:896], in_=acc_2[:])
+        store(768, 896)
+        nc.scalar.copy(out=result[:, 896:1024], in_=acc_3[:])
+        store(896, 1024)

@@ -125,15 +125,36 @@ def tile_autoencoder_pb_s_kernel(tc, z, centers_decoder, alpha_decoder, out):
         zT_m2 = keep.tile([P, SAMPLES], BF16)
         nc.scalar.mul(out=zT_m2[:], in_=zT_ps[:], mul=-2.0)
 
+        scalar_norms = BLOCKS - VECTOR_NORMS
+        cc = keep.tile([P, scalar_norms], F32)
+        ncc_s = keep.tile([P, scalar_norms], F32)
+        ncc_v = keep.tile([P, VECTOR_NORMS], F32)
+        c_sq = keep.tile([P, BLOCKS, LATENT], F32)
+        for b in range(scalar_norms):
+            nc.scalar.activation(
+                out=c_sq[:, b, :], in_=c_sb[:, b, :], func=ACT.Square, accum_out=cc[:, b : b + 1]
+            )
+        nc.scalar.mul(out=ncc_s[:], in_=cc[:], mul=-0.5)
+
+        def vector_norm(b):
+            nc.vector.scalar_tensor_tensor(
+                out=c_sq[:, b, :],
+                in0=c_sb[:, b, :],
+                scalar=-0.5,
+                in1=c_sb[:, b, :],
+                op0=ALU.mult,
+                op1=ALU.mult,
+                accum_out=ncc_v[:, b - scalar_norms : b - scalar_norms + 1],
+            )
+
         cT = keep.tile([P, BLOCKS, P], BF16)
         cT_ps = []
-        for c in range(PASSES):
+        g_ps = []
+
+        def transpose_centres(c):
             cT_ps.append(psum.tile([P, PACK, P], BF16, name="cT_ps_%d" % c))
             for t in range(PACK):
                 nc.tensor.transpose(cT_ps[c][:, t, :], c_sb[:, c * PACK + t, :], ident_bf[:])
-
-        g_ps = []
-        for c in range(PASSES):
             g_ps.append(psum.tile([P, PACK, SAMPLES], F32, name="g_ps_%d" % c))
             for t in range(PACK):
                 nc.tensor.matmul(
@@ -145,30 +166,10 @@ def tile_autoencoder_pb_s_kernel(tc, z, centers_decoder, alpha_decoder, out):
                     is_transpose=True,
                 )
 
-        scalar_norms = BLOCKS - VECTOR_NORMS
-        cc = keep.tile([P, scalar_norms], F32)
-        ncc_s = keep.tile([P, scalar_norms], F32)
-        ncc_v = keep.tile([P, VECTOR_NORMS], F32)
-        c_sq = keep.tile([P, BLOCKS, LATENT], F32)
-        for b in range(scalar_norms):
-            nc.scalar.activation(
-                out=c_sq[:, b, :], in_=c_sb[:, b, :], func=ACT.Square, accum_out=cc[:, b : b + 1]
-            )
-        nc.scalar.mul(out=ncc_s[:], in_=cc[:], mul=-0.5)
-        for b in range(scalar_norms, BLOCKS):
-            nc.vector.scalar_tensor_tensor(
-                out=c_sq[:, b, :],
-                in0=c_sb[:, b, :],
-                scalar=-0.5,
-                in1=c_sb[:, b, :],
-                op0=ALU.mult,
-                op1=ALU.mult,
-                accum_out=ncc_v[:, b - scalar_norms : b - scalar_norms + 1],
-            )
-        for c in range(PASSES):
+        def copy_centres(c):
             nc.vector.tensor_copy(out=cT[:, c * PACK : (c + 1) * PACK, :], in_=cT_ps[c][:])
 
-        for c in range(PASSES):
+        def dot_products(c):
             for t in range(PACK):
                 nc.tensor.matmul(
                     g_ps[c][:, t, :],
@@ -193,25 +194,34 @@ def tile_autoencoder_pb_s_kernel(tc, z, centers_decoder, alpha_decoder, out):
         def store(lo, hi):
             nc.sync.dma_start(out=out[:, lo:hi], in_=result[:, lo:hi])
 
+        vector_norm(scalar_norms)
+        transpose_centres(0)
+        copy_centres(0)
+        dot_products(0)
+        for b in range(scalar_norms + 1, BLOCKS):
+            vector_norm(b)
         regroup_scalar(0)
         regroup_vector(0)
+        transpose_centres(1)
+        copy_centres(1)
+        dot_products(1)
         exp_k(0)
+        exp_k(1)
         regroup_vector(1)
         regroup_scalar(1)
         quantise_alpha(0)
-        exp_k(1)
-        regroup_vector(2)
-        regroup_scalar(2)
-        quantise_alpha(1)
         clamp_and_regroup_k(0)
         clamp_and_regroup_k(1)
-        regroup_vector(3)
-        regroup_scalar(3)
+        regroup_vector(2)
+        regroup_scalar(2)
         nc.vector.quantize_mx(
             out=k_codes[:].rearrange("p c i -> p (c i)").bitcast(FP8X4),
             scales=k_scales[:].rearrange("p c i -> p (c i)"),
             in_=k_grouped[:].rearrange("p c i t -> p (c i t)"),
         )
+        quantise_alpha(1)
+        regroup_vector(3)
+        regroup_scalar(3)
         quantise_alpha(2)
 
         acc_0 = psum.tile([P, 512], F32)

@@ -26,10 +26,10 @@ RUN = 4
 VECTOR_NORMS = 3
 
 UNITS = (
-    (0, 0, 0, 512, 288),
-    (0, 1, 0, 512, 288),
-    (1, 0, 0, 512, 288),
-    (1, 1, 0, 256, 96),
+    (0, 0, 0, 512, 384),
+    (0, 1, 0, 512, 384),
+    (1, 0, 0, 512, 128),
+    (1, 1, 0, 256, 0),
     (1, 1, 256, 512, 256),
 )
 
@@ -206,10 +206,10 @@ def tile_autoencoder_pb_s_kernel(tc, z, centers_decoder, alpha_decoder, out):
         copy_centres(1)
         dot_products(1)
         exp_k(0)
-        exp_k(1)
+        quantise_alpha(0)
         regroup_vector(1)
         regroup_scalar(1)
-        quantise_alpha(0)
+        exp_k(1)
         clamp_and_regroup_k(0)
         clamp_and_regroup_k(1)
         regroup_vector(2)
@@ -220,7 +220,6 @@ def tile_autoencoder_pb_s_kernel(tc, z, centers_decoder, alpha_decoder, out):
             in_=k_grouped[:].rearrange("p c i t -> p (c i t)"),
         )
         quantise_alpha(1)
-        regroup_vector(3)
         regroup_scalar(3)
         quantise_alpha(2)
 

@@ -205,6 +205,14 @@ def tile_autoencoder_pb_s_kernel(tc, z, centers_decoder, alpha_decoder, out):
         transpose_centres(1)
         copy_centres(1)
         dot_products(1)
+        warm_ps = psum.tile([P, 512], F32, tag="bank_w")
+        nc.tensor.matmul(
+            warm_ps[:],
+            lhsT=zero_col[:, 0:1].to_broadcast([P, P]),
+            rhs=zero_col[:, 0:1].to_broadcast([P, 512]),
+            start=True,
+            stop=True,
+        )
         exp_k(0)
         quantise_alpha(0)
         regroup_vector(1)
@@ -223,7 +231,7 @@ def tile_autoencoder_pb_s_kernel(tc, z, centers_decoder, alpha_decoder, out):
         regroup_scalar(3)
         quantise_alpha(2)
 
-        acc_0 = psum.tile([P, 512], F32)
+        acc_0 = psum.tile([P, 512], F32, tag="bank_w")
         multiply(acc_0[:], 0, 0, 0, 512)
         multiply(acc_0[:], 0, 1, 0, 512)
         nc.scalar.copy(out=result[:, 0:512], in_=acc_0[:])

@@ -240,19 +240,14 @@ def tile_autoencoder_pb_s_kernel(tc, z, centers_decoder, alpha_decoder, out):
         regroup_vector(4)
         quantise_alpha(3)
         acc_1 = psum.tile([P, 256], F32)
-        acc_2 = psum.tile([P, 128], F32)
-        acc_3 = psum.tile([P, 128], F32, tag="bank_z")
+        acc_2 = psum.tile([P, 256], F32)
         multiply(acc_1[:], 1, 0, 0, 256)
-        multiply(acc_2[:], 1, 0, 256, 384)
-        multiply(acc_3[:], 1, 0, 384, 512)
+        multiply(acc_2[:], 1, 0, 256, 512)
         multiply(acc_1[:], 1, 1, 0, 256)
         nc.scalar.copy(out=result[:, 512:768], in_=acc_1[:])
         store(512, 768)
 
         quantise_alpha(4)
-        multiply(acc_2[:], 1, 1, 256, 384)
-        multiply(acc_3[:], 1, 1, 384, 512)
-        nc.vector.tensor_copy(out=result[:, 768:896], in_=acc_2[:])
-        store(768, 896)
-        nc.scalar.copy(out=result[:, 896:1024], in_=acc_3[:])
-        store(896, 1024)
+        multiply(acc_2[:], 1, 1, 256, 512)
+        nc.vector.tensor_copy(out=result[:, 768:1024], in_=acc_2[:])
+        store(768, 1024)

@@ -1,7 +1,6 @@
 from contextlib import ExitStack
 
 import concourse.mybir as mybir
-from concourse.masks import make_identity
 
 BF16 = mybir.dt.bfloat16
 F32 = mybir.dt.float32
@@ -12,6 +11,7 @@ ALU = mybir.AluOpType
 ACT = mybir.ActivationFunctionType
 
 P = 128
+BLOCK = 32
 PACK = 4
 K_PASS = P * PACK
 SAMPLES = 128
@@ -108,12 +108,27 @@ def tile_autoencoder_pb_s_kernel(tc, z, centers_decoder, alpha_decoder, out):
                 stop=(c == PASSES - 1),
             )
 
-        ident_bf = keep.tile([P, P], BF16)
-        make_identity(nc, ident_bf[:])
-        ident_f32 = keep.tile([P, P], F32)
-        make_identity(nc, ident_f32[:])
         zero_col = keep.tile([P, 1], F32)
         nc.vector.memset(zero_col[:], 0.0)
+        ones = keep.tile([P, BLOCK], F32)
+        nc.vector.memset(ones[:], 1.0)
+        ident_bf = keep.tile([P, P], BF16)
+        nc.vector.memset(ident_bf[:], 0.0)
+        counts = keep.tile([P, BLOCK], F32, align_bytes=64)
+        nc.vector.tensor_tensor_scan(
+            out=counts[:], data0=ones[:], data1=ones[:], initial=-1.0, op0=ALU.mult, op1=ALU.add
+        )
+        turned = keep.tile([P, BLOCK], F32, align_bytes=64)
+        nc.vector.transpose(out=turned[:], in_=counts[:])
+        for lo in range(0, P, BLOCK):
+            nc.vector.tensor_tensor(
+                out=ident_bf[lo : lo + BLOCK, lo : lo + BLOCK],
+                in0=counts[lo : lo + BLOCK, :],
+                in1=turned[lo : lo + BLOCK, :],
+                op=ALU.is_equal,
+            )
+        ident_f32 = keep.tile([P, P], F32)
+        nc.vector.tensor_copy(out=ident_f32[:], in_=ident_bf[:])
         one_col = keep.tile([P, 1], F32)
         nc.scalar.activation(out=one_col[:], in_=zero_col[:], func=ACT.Exp)
 

@@ -23,6 +23,7 @@ BLOCKS = PASSES * PACK
 F_TILE = 512
 F_TILES = FEATURES // F_TILE
 RUN = 4
+WARM_COLUMNS = 256
 VECTOR_NORMS = 3
 
 UNITS = (
@@ -132,6 +133,18 @@ def tile_autoencoder_pb_s_kernel(tc, z, centers_decoder, alpha_decoder, out):
         one_col = keep.tile([P, 1], F32)
         nc.scalar.activation(out=one_col[:], in_=zero_col[:], func=ACT.Exp)
 
+        def keep_warm():
+            warm_ps = psum.tile([P, WARM_COLUMNS], F32, tag="bank_w")
+            nc.tensor.matmul(
+                warm_ps[:],
+                lhsT=zero_col[:, 0:1].to_broadcast([P, P]),
+                rhs=zero_col[:, 0:1].to_broadcast([P, WARM_COLUMNS]),
+                start=True,
+                stop=True,
+            )
+
+        keep_warm()
+
         zz = keep.tile([P, 1], F32)
         z_sq = keep.tile([P, LATENT], F32)
         nc.scalar.activation(out=z_sq[:], in_=z_sb[:], func=ACT.Square, accum_out=zz[:])
@@ -220,14 +233,7 @@ def tile_autoencoder_pb_s_kernel(tc, z, centers_decoder, alpha_decoder, out):
         transpose_centres(1)
         copy_centres(1)
         dot_products(1)
-        warm_ps = psum.tile([P, 512], F32, tag="bank_w")
-        nc.tensor.matmul(
-            warm_ps[:],
-            lhsT=zero_col[:, 0:1].to_broadcast([P, P]),
-            rhs=zero_col[:, 0:1].to_broadcast([P, 512]),
-            start=True,
-            stop=True,
-        )
+        keep_warm()
         exp_k(0)
         quantise_alpha(0)
         regroup_vector(1)

@@ -31,7 +31,7 @@ UNITS = (
     (0, 1, 0, 512, 384),
     (1, 0, 0, 512, 128),
     (1, 1, 0, 256, 0),
-    (1, 1, 256, 512, 256),
+    (1, 1, 256, 512, 192),
 )
 
 FLOPS = 2 * SAMPLES * LATENT * CENTRES + 2 * SAMPLES * CENTRES * FEATURES
@@ -236,6 +236,17 @@ def tile_autoencoder_pb_s_kernel(tc, z, centers_decoder, alpha_decoder, out):
         keep_warm()
         exp_k(0)
         quantise_alpha(0)
+        warm_mx = psum.tile([P, F_TILE], F32, tag="bank_w")
+        for n in range(2):
+            nc.tensor.matmul_mx(
+                out=warm_mx[:],
+                lhsT=a_codes[:, 0, 0, 0:P].bitcast(FP8X4),
+                lhsT_scale=a_scales[:, 0, 0, 0:P],
+                rhs=a_codes[:, 0, 0, :].bitcast(FP8X4),
+                rhs_scale=a_scales[:, 0, 0, :],
+                start=True,
+                stop=True,
+            )
         regroup_vector(1)
         regroup_scalar(1)
         exp_k(1)
@@ -250,6 +261,7 @@ def tile_autoencoder_pb_s_kernel(tc, z, centers_decoder, alpha_decoder, out):
         )
         quantise_alpha(1)
         regroup_scalar(3)
+        regroup_scalar(4)
         quantise_alpha(2)
 
         acc_0 = psum.tile([P, 512], F32, tag="bank_w")

@@ -30,8 +30,8 @@ UNITS = (
     (0, 0, 0, 512, 384),
     (0, 1, 0, 512, 384),
     (1, 0, 0, 512, 128),
-    (1, 1, 0, 256, 0),
-    (1, 1, 256, 512, 192),
+    (1, 1, 0, 256, 64),
+    (1, 1, 256, 512, 160),
 )
 
 FLOPS = 2 * SAMPLES * LATENT * CENTRES + 2 * SAMPLES * CENTRES * FEATURES
@@ -71,14 +71,13 @@ def tile_autoencoder_pb_s_kernel(tc, z, centers_decoder, alpha_decoder, out):
                     "(p t) l -> p (t l)", t=PACK
                 ),
             )
-        for f in range(F_TILES):
-            for c in range(PASSES):
-                nc.sync.dma_start(
-                    out=a_rows[:, f, c, :, :],
-                    in_=alpha_decoder[
-                        c * K_PASS : (c + 1) * K_PASS, f * F_TILE : (f + 1) * F_TILE
-                    ].rearrange("(p t) w -> p t w", t=PACK),
-                )
+        for f, c, lo, hi in ((0, 0, 0, 512), (0, 1, 0, 512), (1, 0, 0, 512), (1, 1, 0, 256), (1, 1, 256, 512)):
+            nc.sync.dma_start(
+                out=a_rows[:, f, c, :, lo:hi],
+                in_=alpha_decoder[
+                    c * K_PASS : (c + 1) * K_PASS, f * F_TILE + lo : f * F_TILE + hi
+                ].rearrange("(p t) w -> p t w", t=PACK),
+            )
 
         def regroup_vector(u):
             f, c, lo, hi, v = UNITS[u]
@@ -262,6 +261,7 @@ def tile_autoencoder_pb_s_kernel(tc, z, centers_decoder, alpha_decoder, out):
         quantise_alpha(1)
         regroup_scalar(3)
         regroup_scalar(4)
+        regroup_vector(3)
         quantise_alpha(2)
 
         acc_0 = psum.tile([P, 512], F32, tag="bank_w")

@@ -31,7 +31,8 @@ UNITS = (
     (0, 1, 0, 512, 384),
     (1, 0, 0, 512, 128),
     (1, 1, 0, 256, 64),
-    (1, 1, 256, 512, 160),
+    (1, 1, 256, 384, 32),
+    (1, 1, 384, 512, 128),
 )
 
 FLOPS = 2 * SAMPLES * LATENT * CENTRES + 2 * SAMPLES * CENTRES * FEATURES
@@ -271,16 +272,24 @@ def tile_autoencoder_pb_s_kernel(tc, z, centers_decoder, alpha_decoder, out):
         store(0, 512)
 
         regroup_vector(4)
+        regroup_vector(5)
         quantise_alpha(3)
         acc_1 = psum.tile([P, 256], F32)
-        acc_2 = psum.tile([P, 256], F32)
+        acc_2 = psum.tile([P, 128], F32)
+        acc_3 = psum.tile([P, 128], F32, tag="bank_z")
         multiply(acc_1[:], 1, 0, 0, 256)
-        multiply(acc_2[:], 1, 0, 256, 512)
+        multiply(acc_2[:], 1, 0, 256, 384)
+        multiply(acc_3[:], 1, 0, 384, 512)
         multiply(acc_1[:], 1, 1, 0, 256)
         nc.scalar.copy(out=result[:, 512:768], in_=acc_1[:])
         store(512, 768)
 
         quantise_alpha(4)
-        multiply(acc_2[:], 1, 1, 256, 512)
-        nc.vector.tensor_copy(out=result[:, 768:1024], in_=acc_2[:])
-        store(768, 1024)
+        multiply(acc_2[:], 1, 1, 256, 384)
+        nc.scalar.copy(out=result[:, 768:896], in_=acc_2[:])
+        store(768, 896)
+
+        quantise_alpha(5)
+        multiply(acc_3[:], 1, 1, 384, 512)
+        nc.vector.tensor_copy(out=result[:, 896:1024], in_=acc_3[:])
+        store(896, 1024)

from contextlib import ExitStack

import concourse.mybir as mybir

BF16 = mybir.dt.bfloat16
F32 = mybir.dt.float32
U32 = mybir.dt.uint32
U8 = mybir.dt.uint8
FP8X4 = mybir.dt.float8_e4m3fn_x4
ALU = mybir.AluOpType
ACT = mybir.ActivationFunctionType

P = 128
BLOCK = 32
PACK = 4
K_PASS = P * PACK
SAMPLES = 128
LATENT = 128
CENTRES = 1024
FEATURES = 1024
PASSES = CENTRES // K_PASS
BLOCKS = PASSES * PACK
F_TILE = 512
F_TILES = FEATURES // F_TILE
RUN = 4
WARM_COLUMNS = 256
VECTOR_NORMS = 3

UNITS = (
    (0, 0, 0, 512, 384),
    (0, 1, 0, 512, 384),
    (1, 0, 0, 512, 128),
    (1, 1, 0, 256, 64),
    (1, 1, 256, 384, 32),
    (1, 1, 384, 512, 128),
)

FLOPS = 2 * SAMPLES * LATENT * CENTRES + 2 * SAMPLES * CENTRES * FEATURES


def side_by_side(rows, grouped):
    return (
        rows.rearrange("p t (w i) -> p w t i", i=RUN),
        grouped.rearrange("p (w i) t -> p w t i", i=RUN),
    )


def tile_autoencoder_pb_s_kernel(tc, z, centers_decoder, alpha_decoder, out):
    nc = tc.nc
    with ExitStack() as ctx:
        keep = ctx.enter_context(tc.tile_pool(name="keep", bufs=1))
        psum = ctx.enter_context(tc.psum_pool(name="psum", bufs=1))
        ctx.enter_context(tc.manual_schedule())

        z_sb = keep.tile([P, LATENT], BF16)
        c_sb = keep.tile([P, BLOCKS, LATENT], BF16)
        a_rows = keep.tile([P, F_TILES, PASSES, PACK, F_TILE], BF16)
        a_grouped = keep.tile([P, F_TILES, PASSES, F_TILE, PACK], BF16, align_bytes=64)
        a_codes = keep.tile([P, F_TILES, PASSES, F_TILE], U32, align_bytes=64)
        a_scales = keep.tile([P, F_TILES, PASSES, F_TILE], U8, align_bytes=64)
        k_rows = keep.tile([P, PASSES, PACK, SAMPLES], BF16)
        k_grouped = keep.tile([P, PASSES, SAMPLES, PACK], BF16, align_bytes=64)
        k_codes = keep.tile([P, PASSES, SAMPLES], U32, align_bytes=64)
        k_scales = keep.tile([P, PASSES, SAMPLES], U8, align_bytes=64)
        result = keep.tile([P, FEATURES], F32)

        nc.sync.dma_start(out=z_sb[:], in_=z)
        for c in range(PASSES):
            nc.sync.dma_start(
                out=c_sb[:, c * PACK : (c + 1) * PACK, :].rearrange("p t l -> p (t l)"),
                in_=centers_decoder[c * K_PASS : (c + 1) * K_PASS, :].rearrange(
                    "(p t) l -> p (t l)", t=PACK
                ),
            )
        for f, c, lo, hi in ((0, 0, 0, 512), (0, 1, 0, 512), (1, 0, 0, 512), (1, 1, 0, 256), (1, 1, 256, 512)):
            nc.sync.dma_start(
                out=a_rows[:, f, c, :, lo:hi],
                in_=alpha_decoder[
                    c * K_PASS : (c + 1) * K_PASS, f * F_TILE + lo : f * F_TILE + hi
                ].rearrange("(p t) w -> p t w", t=PACK),
            )

        def regroup_vector(u):
            f, c, lo, hi, v = UNITS[u]
            src, dst = side_by_side(a_rows[:, f, c, :, lo : lo + v], a_grouped[:, f, c, lo : lo + v, :])
            nc.vector.tensor_copy(out=dst, in_=src)

        def regroup_scalar(u):
            f, c, lo, hi, v = UNITS[u]
            src, dst = side_by_side(a_rows[:, f, c, :, lo + v : hi], a_grouped[:, f, c, lo + v : hi, :])
            nc.scalar.copy(out=dst, in_=src)

        def quantise_alpha(u):
            f, c, lo, hi, v = UNITS[u]
            nc.vector.quantize_mx(
                out=a_codes[:, f, c, lo:hi].bitcast(FP8X4),
                scales=a_scales[:, f, c, lo:hi],
                in_=a_grouped[:, f, c, lo:hi, :].rearrange("p w t -> p (w t)"),
            )

        def multiply(acc, f, c, lo, hi):
            nc.tensor.matmul_mx(
                out=acc,
                lhsT=k_codes[:, c, :].bitcast(FP8X4),
                lhsT_scale=k_scales[:, c, :],
                rhs=a_codes[:, f, c, lo:hi].bitcast(FP8X4),
                rhs_scale=a_scales[:, f, c, lo:hi],
                start=(c == 0),
                stop=(c == PASSES - 1),
            )

        zero_col = keep.tile([P, 1], F32)
        nc.vector.memset(zero_col[:], 0.0)
        ones = keep.tile([P, BLOCK], F32)
        nc.vector.memset(ones[:], 1.0)
        ident_bf = keep.tile([P, P], BF16)
        nc.vector.memset(ident_bf[:], 0.0)
        counts = keep.tile([P, BLOCK], F32, align_bytes=64)
        nc.vector.tensor_tensor_scan(
            out=counts[:], data0=ones[:], data1=ones[:], initial=-1.0, op0=ALU.mult, op1=ALU.add
        )
        turned = keep.tile([P, BLOCK], F32, align_bytes=64)
        nc.vector.transpose(out=turned[:], in_=counts[:])
        for lo in range(0, P, BLOCK):
            nc.vector.tensor_tensor(
                out=ident_bf[lo : lo + BLOCK, lo : lo + BLOCK],
                in0=counts[lo : lo + BLOCK, :],
                in1=turned[lo : lo + BLOCK, :],
                op=ALU.is_equal,
            )
        ident_f32 = keep.tile([P, P], F32)
        nc.vector.tensor_copy(out=ident_f32[:], in_=ident_bf[:])
        one_col = keep.tile([P, 1], F32)
        nc.scalar.activation(out=one_col[:], in_=zero_col[:], func=ACT.Exp)

        def keep_warm():
            warm_ps = psum.tile([P, WARM_COLUMNS], F32, tag="bank_w")
            nc.tensor.matmul(
                warm_ps[:],
                lhsT=zero_col[:, 0:1].to_broadcast([P, P]),
                rhs=zero_col[:, 0:1].to_broadcast([P, WARM_COLUMNS]),
                start=True,
                stop=True,
            )

        keep_warm()

        zz = keep.tile([P, 1], F32)
        z_sq = keep.tile([P, LATENT], F32)
        nc.scalar.activation(out=z_sq[:], in_=z_sb[:], func=ACT.Square, accum_out=zz[:])
        zT_ps = psum.tile([P, SAMPLES], BF16, tag="bank_z")
        nc.tensor.transpose(zT_ps[:], z_sb[:], ident_bf[:])
        zT_m2 = keep.tile([P, SAMPLES], BF16)
        nc.scalar.mul(out=zT_m2[:], in_=zT_ps[:], mul=-2.0)

        scalar_norms = BLOCKS - VECTOR_NORMS
        cc = keep.tile([P, scalar_norms], F32)
        ncc_s = keep.tile([P, scalar_norms], F32)
        ncc_v = keep.tile([P, VECTOR_NORMS], F32)
        c_sq = keep.tile([P, BLOCKS, LATENT], F32)
        for b in range(scalar_norms):
            nc.scalar.activation(
                out=c_sq[:, b, :], in_=c_sb[:, b, :], func=ACT.Square, accum_out=cc[:, b : b + 1]
            )
        nc.scalar.mul(out=ncc_s[:], in_=cc[:], mul=-0.5)

        def vector_norm(b):
            nc.vector.scalar_tensor_tensor(
                out=c_sq[:, b, :],
                in0=c_sb[:, b, :],
                scalar=-0.5,
                in1=c_sb[:, b, :],
                op0=ALU.mult,
                op1=ALU.mult,
                accum_out=ncc_v[:, b - scalar_norms : b - scalar_norms + 1],
            )

        cT = keep.tile([P, BLOCKS, P], BF16)
        cT_ps = []
        g_ps = []

        def transpose_centres(c):
            cT_ps.append(psum.tile([P, PACK, P], BF16, name="cT_ps_%d" % c))
            for t in range(PACK):
                nc.tensor.transpose(cT_ps[c][:, t, :], c_sb[:, c * PACK + t, :], ident_bf[:])
            g_ps.append(psum.tile([P, PACK, SAMPLES], F32, name="g_ps_%d" % c))
            for t in range(PACK):
                nc.tensor.matmul(
                    g_ps[c][:, t, :],
                    lhsT=zz[:, 0:1].to_broadcast([P, P]),
                    rhs=ident_f32[:],
                    start=(t == 0),
                    stop=False,
                    is_transpose=True,
                )

        def copy_centres(c):
            nc.vector.tensor_copy(out=cT[:, c * PACK : (c + 1) * PACK, :], in_=cT_ps[c][:])

        def dot_products(c):
            for t in range(PACK):
                nc.tensor.matmul(
                    g_ps[c][:, t, :],
                    lhsT=cT[:, c * PACK + t, :],
                    rhs=zT_m2[:],
                    start=False,
                    stop=(t == PACK - 1),
                )

        def exp_k(c):
            for t in range(PACK):
                b = c * PACK + t
                bias = ncc_s[:, b : b + 1] if b < scalar_norms else ncc_v[:, b - scalar_norms : b - scalar_norms + 1]
                nc.scalar.activation(
                    out=k_rows[:, c, t, :], in_=g_ps[c][:, t, :], func=ACT.Exp, scale=-0.5, bias=bias
                )

        def clamp_and_regroup_k(c):
            src, dst = side_by_side(k_rows[:, c, :, :], k_grouped[:, c, :, :])
            nc.vector.tensor_scalar_min(out=dst, in0=src, scalar1=1.0)

        def store(lo, hi):
            nc.sync.dma_start(out=out[:, lo:hi], in_=result[:, lo:hi])

        vector_norm(scalar_norms)
        transpose_centres(0)
        copy_centres(0)
        dot_products(0)
        for b in range(scalar_norms + 1, BLOCKS):
            vector_norm(b)
        regroup_scalar(0)
        regroup_vector(0)
        transpose_centres(1)
        copy_centres(1)
        dot_products(1)
        keep_warm()
        exp_k(0)
        quantise_alpha(0)
        warm_mx = psum.tile([P, F_TILE], F32, tag="bank_w")
        for n in range(2):
            nc.tensor.matmul_mx(
                out=warm_mx[:],
                lhsT=a_codes[:, 0, 0, 0:P].bitcast(FP8X4),
                lhsT_scale=a_scales[:, 0, 0, 0:P],
                rhs=a_codes[:, 0, 0, :].bitcast(FP8X4),
                rhs_scale=a_scales[:, 0, 0, :],
                start=True,
                stop=True,
            )
        regroup_vector(1)
        regroup_scalar(1)
        exp_k(1)
        clamp_and_regroup_k(0)
        clamp_and_regroup_k(1)
        regroup_vector(2)
        regroup_scalar(2)
        nc.vector.quantize_mx(
            out=k_codes[:].rearrange("p c i -> p (c i)").bitcast(FP8X4),
            scales=k_scales[:].rearrange("p c i -> p (c i)"),
            in_=k_grouped[:].rearrange("p c i t -> p (c i t)"),
        )
        quantise_alpha(1)
        regroup_scalar(3)
        regroup_scalar(4)
        regroup_vector(3)
        quantise_alpha(2)

        acc_0 = psum.tile([P, 512], F32, tag="bank_w")
        multiply(acc_0[:], 0, 0, 0, 512)
        multiply(acc_0[:], 0, 1, 0, 512)
        nc.scalar.copy(out=result[:, 0:512], in_=acc_0[:])
        store(0, 512)

        regroup_vector(4)
        regroup_vector(5)
        quantise_alpha(3)
        acc_1 = psum.tile([P, 256], F32)
        acc_2 = psum.tile([P, 128], F32)
        acc_3 = psum.tile([P, 128], F32, tag="bank_z")
        multiply(acc_1[:], 1, 0, 0, 256)
        multiply(acc_2[:], 1, 0, 256, 384)
        multiply(acc_3[:], 1, 0, 384, 512)
        multiply(acc_1[:], 1, 1, 0, 256)
        nc.scalar.copy(out=result[:, 512:768], in_=acc_1[:])
        store(512, 768)

        quantise_alpha(4)
        multiply(acc_2[:], 1, 1, 256, 384)
        nc.scalar.copy(out=result[:, 768:896], in_=acc_2[:])
        store(768, 896)

        quantise_alpha(5)
        multiply(acc_3[:], 1, 1, 384, 512)
        nc.vector.tensor_copy(out=result[:, 896:1024], in_=acc_3[:])
        store(896, 1024)
